import numpy as np
import ml_dtypes


def mxq(x, axis, fmt="e4m3"):
    dtype, down = {"e4m3": (ml_dtypes.float8_e4m3fn, 7), "e5m2": (ml_dtypes.float8_e5m2, 14)}[fmt]
    v = np.moveaxis(np.asarray(x, np.float32).astype(ml_dtypes.bfloat16).astype(np.float64), axis, -1)
    blocks = v.reshape(v.shape[:-1] + (-1, 32))
    amax = np.abs(blocks).max(-1, keepdims=True)
    byte = np.maximum(np.where(amax > 0, np.frexp(amax)[1] - 1 + 127, 0) - down, 1)
    scale = np.exp2(byte - 127.0)
    codes = (blocks / scale).astype(np.float32).astype(dtype).astype(np.float64)
    return np.moveaxis((codes * scale).reshape(v.shape), -1, axis)


WIDE = False


def mx_kscale(k):
    if not WIDE:
        return np.ones(k)
    levels = np.array([10, -10, 5, -5, 0])
    if k % 512:
        return np.exp2(np.random.permutation(np.resize(levels, k // 32))).repeat(32)
    a = np.empty((k // 512, 16))
    for p in range(k // 512):
        a[p, :8] = np.random.permutation(np.resize(levels, 8))
        for g in range(8):
            far = levels[np.abs(levels - a[p, g]) >= 10]
            a[p, g + 8] = far[np.random.randint(len(far))]
    return np.exp2(a.ravel()).repeat(32)


BF16 = ml_dtypes.bfloat16


def bf(x):
    return np.asarray(x, np.float32).astype(BF16)


def f64(x):
    return np.asarray(x).astype(np.float64)


BH, S, D = 16, 512, 256
ALPHA = 0.99
EPS = 1e-10
LOG_DECAY = np.log(ALPHA ** np.arange(S - 1.0, -1.0, -1.0) + EPS)


def setup_inputs():
    s = mx_kscale(S)
    decay = np.exp(LOG_DECAY)
    c = (decay * s).sum() / decay.sum()
    a = 1.2 / D ** 0.25
    return {"q": bf(np.random.standard_normal((BH, S, D)) * a),
            "k": bf(np.random.standard_normal((BH, S, D)) * a),
            "v": bf(np.random.standard_normal((BH, S, D)) * 2.0 * c / s[:, None]),
            "attn_mask": bf(np.random.standard_normal((BH, S, S)) * 0.5 + np.log(s))}


def reference(q, k, v, attn_mask):
    scores = f64(q) @ f64(k).transpose(0, 2, 1) + f64(attn_mask)
    scores = scores + LOG_DECAY[None, None, :]
    e = np.exp(scores - scores.max(-1, keepdims=True))
    return (mxq(e, 2, "e4m3") @ mxq(f64(v), 1, "e4m3")) / e.sum(-1, keepdims=True)

@@ -1,0 +1,347 @@
+import math
+from contextlib import ExitStack
+
+import concourse.mybir as mybir
+from concourse.masks import make_identity
+
+F32 = mybir.dt.float32
+BF16 = mybir.dt.bfloat16
+I32 = mybir.dt.int32
+U32 = mybir.dt.uint32
+U8 = mybir.dt.uint8
+FP8X4 = mybir.dt.float8_e4m3fn_x4
+ADD = mybir.AluOpType.add
+MULT = mybir.AluOpType.mult
+MAX = mybir.AluOpType.max
+EXP = mybir.ActivationFunctionType.Exp
+COPY = mybir.ActivationFunctionType.Copy
+AX_X = mybir.AxisListType.X
+
+P = 128
+BH, S, D = 16, 512, 256
+NT = S // P
+NTILES = BH * NT
+NPAIRS = NTILES // 2
+ALPHA = 0.99
+EPS = 1e-10
+LN_ALPHA = math.log(ALPHA)
+C_HI = round(LN_ALPHA * 2097152.0) / 2097152.0
+C_LO = LN_ALPHA - C_HI
+FLOPS = 2 * 2 * BH * S * S * D
+
+LA = 3
+XMODE = "g"
+PIN = True
+PEMASK = tuple(range(2, 62, 5))
+TAILS = 1
+
+
+def tile_dotproductattention_t_kernel(tc, q, k, v, attn_mask, out):
+    nc = tc.nc
+    with ExitStack() as ctx:
+        const = ctx.enter_context(tc.tile_pool(name="const", bufs=1))
+        ld = ctx.enter_context(tc.tile_pool(name="ld", bufs=LA + 1))
+        wk = ctx.enter_context(tc.tile_pool(name="wk", bufs=2))
+        ps_tr = ctx.enter_context(tc.psum_pool(name="ps_tr", bufs=1))
+        ps_s = ctx.enter_context(tc.psum_pool(name="ps_s", bufs=4))
+        ps_et = ctx.enter_context(tc.psum_pool(name="ps_et", bufs=2))
+        ps_o = ctx.enter_context(tc.psum_pool(name="ps_o", bufs=1))
+        if PIN:
+            ctx.enter_context(tc.manual_schedule())
+
+        ident32 = const.tile([P, P], F32)
+        make_identity(nc, ident32[:])
+        identb = const.tile([P, P], BF16)
+        make_identity(nc, identb[:])
+
+        j_i = const.tile([P, NT], I32)
+        nc.gpsimd.iota(j_i[:], pattern=[[1, NT]], base=0, channel_multiplier=NT)
+        j_f = const.tile([P, NT], F32)
+        nc.vector.tensor_copy(out=j_f[:], in_=j_i[:])
+        n_f = const.tile([P, NT], F32)
+        nc.vector.tensor_scalar(out=n_f[:], in0=j_f[:], scalar1=-1.0, scalar2=float(S - 1), op0=MULT, op1=ADD)
+        grow = const.tile([P, NT], F32)
+        nc.scalar.activation(out=grow[:], in_=n_f[:], func=EXP, scale=-LN_ALPHA)
+        low = const.tile([P, NT], F32)
+        nc.vector.tensor_scalar(out=low[:], in0=n_f[:], scalar1=C_LO, scalar2=None, op0=MULT)
+        low2 = const.tile([P, NT], F32)
+        nc.vector.scalar_tensor_tensor(out=low2[:], in0=grow[:], scalar=EPS, in1=low[:], op0=MULT, op1=ADD)
+        dcol = const.tile([P, NT], F32)
+        nc.vector.scalar_tensor_tensor(out=dcol[:], in0=n_f[:], scalar=C_HI, in1=low2[:], op0=MULT, op1=ADD)
+
+        hd = {}
+        pr = {}
+        tl = {}
+
+        def load(h):
+            if h < 0 or h >= BH:
+                return
+            q_sb = ld.tile([P, NT * D], BF16, tag="q", name="q_sb")
+            nc.sync.dma_start(out=q_sb[:], in_=q[h].rearrange("(p t) d -> p (t d)", t=NT))
+            k_sb = ld.tile([P, NT * D], BF16, tag="k", name="k_sb")
+            nc.sync.dma_start(out=k_sb[:], in_=k[h].rearrange("(p t) d -> p (t d)", t=NT))
+            m_sb = ld.tile([P, NT * S], BF16, tag="m", name="m_sb")
+            nc.sync.dma_start(out=m_sb[:], in_=attn_mask[h].rearrange("(p t) j -> p (t j)", t=NT))
+            v_sb = ld.tile([P, NT * D], BF16, tag="v", name="v_sb")
+            nc.sync.dma_start(out=v_sb[:], in_=v[h].rearrange("(p t) d -> p (t d)", t=NT))
+            hd[h] = {"q": q_sb, "k": k_sb, "m": m_sb, "v": v_sb}
+
+        def tqk(h, which):
+            if h < 0 or h >= BH:
+                return
+            src = hd[h][which][:].bitcast(F32)
+            if h == 0 and which == "k":
+                t_ps = ps_o.tile([P, S], F32, tag="o", name="t_ps0")
+            else:
+                t_ps = ps_tr.tile([P, S], F32, tag="tr", name="t_ps")
+            for t in range(NT):
+                nc.tensor.transpose(t_ps[:, t * P:(t + 1) * P], src[:, t * P:(t + 1) * P], ident32[:])
+            hd[h][which + "ps"] = t_ps
+
+        def xq(h):
+            if h < 0 or h >= BH:
+                return
+            qT = wk.tile([P, S], F32, tag="qT", name="qT", bufs=2)
+            nc.scalar.copy(out=qT[:], in_=hd[h]["qps"][:])
+            hd[h]["qTb"] = qT[:].bitcast(BF16).rearrange("w (t p e) -> w t p e", t=NT, e=2)
+
+        def xk(h):
+            if h < 0 or h >= BH:
+                return
+            kT = wk.tile([P, S], F32, tag="kT", name="kT", bufs=2)
+            if h == 0:
+                nc.vector.tensor_copy(out=kT[:], in_=hd[h]["kps"][:])
+            else:
+                nc.scalar.copy(out=kT[:], in_=hd[h]["kps"][:])
+            hd[h]["kTb"] = kT[:].bitcast(BF16).rearrange("w (j e) -> w j e", e=2)
+
+        def rgv(h):
+            if h < 0 or h >= BH:
+                return
+            vg = wk.tile([P, D * NT], BF16, tag="vg", name="vg", align_bytes=64, bufs=2)
+            nc.vector.tensor_copy(
+                out=vg[:].rearrange("p (c i t) -> p c t i", i=4, t=NT),
+                in_=hd[h]["v"][:].rearrange("p (t c i) -> p c t i", t=NT, i=4),
+            )
+            hd[h]["vg"] = vg
+
+        def qv(h):
+            if h < 0 or h >= BH:
+                return
+            vcod = wk.tile([P, D], U32, tag="vcod", name="vcod", align_bytes=64, bufs=3)
+            vscl = wk.tile([P, D], U8, tag="vscl", name="vscl", align_bytes=64, bufs=3)
+            nc.vector.quantize_mx(out=vcod[:].bitcast(FP8X4), scales=vscl[:], in_=hd[h]["vg"][:])
+            hd[h]["vcod"] = vcod
+            hd[h]["vscl"] = vscl
+
+        def mview(kk):
+            t = kk % NT
+            return hd[kk // NT]["m"][:, t * S:(t + 1) * S].rearrange("i (p c) -> i c p", c=NT)
+
+        def cview(ap):
+            return ap.rearrange("i (c p) -> i c p", c=NT)
+
+        def mm(kq, e):
+            if kq < 0 or kq >= NTILES:
+                return
+            st = hd[kq // NT]
+            t = kq % NT
+            if e == 0:
+                s_new = ps_s.tile([P, S], F32, tag="s", name="s_ps")
+                tl[kq] = {"s_ps": s_new}
+            s_ps = tl[kq]["s_ps"]
+            nc.tensor.matmul(s_ps[:], lhsT=st["qTb"][:, t, :, e], rhs=st["kTb"][:, :, e], start=(e == 0), stop=False)
+            if e == 1 and kq in PEMASK:
+                nc.tensor.matmul(cview(s_ps[:]), lhsT=identb[:], rhs=mview(kq), start=False, stop=False)
+
+        def dec(kq, cs):
+            if kq < 0 or kq >= NTILES:
+                return
+            s_ps = tl[kq]["s_ps"]
+            for c in cs:
+                nc.tensor.matmul(
+                    s_ps[:, c * P:(c + 1) * P],
+                    lhsT=dcol[:, c:c + 1].to_broadcast([P, P]),
+                    rhs=ident32[:],
+                    start=False,
+                    stop=(c == NT - 1),
+                    is_transpose=True,
+                )
+
+        def etr(ke, cs):
+            if ke < 0 or ke >= NTILES:
+                return
+            n = ke // 2
+            a = ke % 2
+            if a == 0 and cs[0] == 0:
+                eT_new = ps_et.tile([P, 2, NT, P], BF16, tag="et", name="eT_ps")
+                pr[n]["eT_ps"] = eT_new
+            for c in cs:
+                nc.tensor.transpose(pr[n]["eT_ps"][:, a, c, :], tl[ke]["e_sb"][:, c * P:(c + 1) * P], identb[:])
+
+        def badd(kk):
+            if kk < 0 or kk >= NTILES:
+                return
+            if kk in PEMASK:
+                tl[kk]["s_src"] = tl[kk]["s_ps"]
+            else:
+                s_sb = wk.tile([P, S], F32, tag="s_sb", name="s_sb", bufs=5)
+                nc.vector.tensor_tensor(out=cview(s_sb[:]), in0=cview(tl[kk]["s_ps"][:]), in1=mview(kk), op=ADD)
+                tl[kk]["s_src"] = s_sb
+
+        def cmax(kk):
+            if kk < 0 or kk >= NTILES:
+                return
+            negm = wk.tile([P, 1], F32, tag="negm", name="negm", bufs=4)
+            nc.vector.tensor_reduce(out=negm[:], in_=tl[kk]["s_src"][:], axis=AX_X, op=MAX, negate=True)
+            tl[kk]["negm"] = negm
+
+        def dexp(kk):
+            if kk < 0 or kk >= NTILES:
+                return
+            n = kk // 2
+            a = kk % 2
+            if n not in pr:
+                rsum_new = wk.tile([P, 2], F32, tag="rsum", name="rsum", bufs=6)
+                pr[n] = {"rsum": rsum_new}
+            e_sb = wk.tile([P, S], BF16, tag="e_sb", name="e_sb", bufs=4)
+            nc.scalar.activation(
+                out=e_sb[:], in_=tl[kk]["s_src"][:], func=EXP, bias=tl[kk]["negm"][:], scale=1.0,
+                accum_out=pr[n]["rsum"][:, a:a + 1],
+            )
+            tl[kk]["e_sb"] = e_sb
+
+        def xe(n):
+            if n < 0 or n >= NPAIRS:
+                return
+            grp = wk.tile([P, 2 * P * NT], BF16, tag="grp", name="grp", align_bytes=64, bufs=1)
+            if XMODE == "g" and n < NPAIRS - TAILS:
+                etc = wk.tile([P, 2 * NT * P], BF16, tag="etc", name="etc", bufs=3)
+                nc.scalar.copy(out=etc[:], in_=pr[n]["eT_ps"][:].rearrange("p a c i -> p (a c i)"))
+                nc.gpsimd.tensor_scalar(
+                    out=grp[:].rearrange("p (a i c) -> p a i c", a=2, c=NT),
+                    in0=etc[:].rearrange("p (a c i) -> p a i c", a=2, c=NT),
+                    scalar1=1.0, scalar2=0.0, op0=MULT, op1=ADD,
+                )
+            else:
+                nc.scalar.copy(
+                    out=grp[:].rearrange("p (a i c) -> p a i c", a=2, c=NT),
+                    in_=pr[n]["eT_ps"][:].rearrange("p a c i -> p a i c"),
+                )
+            pr[n]["grp"] = grp
+
+        def qe(n):
+            if n < 0 or n >= NPAIRS:
+                return
+            ecod = wk.tile([P, 2 * P], U32, tag="ecod", name="ecod", align_bytes=64, bufs=3)
+            escl = wk.tile([P, 2 * P], U8, tag="escl", name="escl", align_bytes=64, bufs=3)
+            nc.vector.quantize_mx(out=ecod[:].bitcast(FP8X4), scales=escl[:], in_=pr[n]["grp"][:])
+            rinv = wk.tile([P, 2], F32, tag="rinv", name="rinv", bufs=4)
+            nc.vector.reciprocal(rinv[:], pr[n]["rsum"][:])
+            pr[n]["ecod"] = ecod
+            pr[n]["escl"] = escl
+            pr[n]["rinv"] = rinv
+
+        def pv(n):
+            if n < 0 or n >= NPAIRS:
+                return
+            st = hd[n // 2]
+            o_ps = ps_o.tile([P, 2, D], F32, tag="o", name="o_ps")
+            for a in range(2):
+                nc.tensor.matmul_mx(
+                    out=o_ps[:, a, :],
+                    lhsT=pr[n]["ecod"][:, a * P:(a + 1) * P].bitcast(FP8X4),
+                    lhsT_scale=pr[n]["escl"][:, a * P:(a + 1) * P],
+                    rhs=st["vcod"][:].bitcast(FP8X4),
+                    rhs_scale=st["vscl"][:],
+                    start=True,
+                    stop=True,
+                )
+            pr[n]["o_ps"] = o_ps
+
+        def oex(kk):
+            if kk < 0 or kk >= NTILES:
+                return
+            h = kk // NT
+            t = kk % NT
+            n = kk // 2
+            a = kk % 2
+            if t == 0:
+                o_new = wk.tile([P, NT * D], F32, tag="o_sb", name="o_sb", bufs=3)
+                hd[h]["o_sb"] = o_new
+            o_sb = hd[h]["o_sb"]
+            if n % 4 == 3:
+                nc.vector.tensor_scalar(
+                    out=o_sb[:, t * D:(t + 1) * D], in0=pr[n]["o_ps"][:, a, :], scalar1=pr[n]["rinv"][:, a:a + 1],
+                    scalar2=None, op0=MULT,
+                )
+            else:
+                nc.scalar.activation(
+                    out=o_sb[:, t * D:(t + 1) * D], in_=pr[n]["o_ps"][:, a, :], func=COPY,
+                    scale=pr[n]["rinv"][:, a:a + 1],
+                )
+
+        def store(h):
+            if h < 0 or h >= BH:
+                return
+            nc.sync.dma_start(out=out[h].rearrange("(p t) d -> p (t d)", t=NT), in_=hd[h]["o_sb"][:])
+
+        def store_half(h, half):
+            nc.sync.dma_start(
+                out=out[h].rearrange("(p t) d -> p (t d)", t=NT)[:, half * 2 * D:(half + 1) * 2 * D],
+                in_=hd[h]["o_sb"][:, half * 2 * D:(half + 1) * 2 * D],
+            )
+
+        for h in range(LA):
+            load(h)
+        for s in range(-8, NTILES + 13):
+            if s >= 0 and s % 4 == 0:
+                load(s // 4 + LA)
+            if (s - 11) % 4 == 0 and (s - 11) // 4 < BH - 1:
+                store((s - 11) // 4)
+            if s == NTILES + 5:
+                store_half(BH - 1, 0)
+            if s == NTILES + 7:
+                store_half(BH - 1, 1)
+            mm(s + 3, 0)
+            dec(s + 2, (0, 1))
+            etr(s - 2, (0, 1))
+            mm(s + 3, 1)
+            dec(s + 2, (2, 3))
+            etr(s - 2, (2, 3))
+            if (s + 8) % 4 == 0:
+                tqk((s + 8) // 4, "q")
+            if s == -8:
+                tqk(0, "k")
+            if (s + 6) % 4 == 0 and s > -6:
+                tqk((s + 6) // 4, "k")
+            if (s - 7) % 2 == 0:
+                pv((s - 7) // 2)
+            if s == -7:
+                xk(0)
+            if s + 1 in PEMASK:
+                badd(s + 1)
+                cmax(s + 1)
+            else:
+                badd(s + 1)
+            if s not in PEMASK:
+                cmax(s)
+            if (s - 2) % 4 == 0:
+                rgv((s - 2) // 4)
+            if (s - 4) % 4 == 0:
+                qv((s - 4) // 4)
+            if (s - 6) % 2 == 0:
+                qe((s - 6) // 2)
+            if s in PEMASK:
+                dexp(s)
+            if s - 1 not in PEMASK:
+                dexp(s - 1)
+            if (s - 4) % 2 == 0:
+                xe((s - 4) // 2)
+            if (s - 8) % 2 == 0:
+                oex(s - 8)
+                oex(s - 7)
+            if (s + 7) % 4 == 0:
+                xq((s + 7) // 4)
+            if (s + 5) % 4 == 0 and s > -5:
+                xk((s + 5) // 4)

@@ -13,6 +13,7 @@ FP8X4 = mybir.dt.float8_e4m3fn_x4
 ADD = mybir.AluOpType.add
 MULT = mybir.AluOpType.mult
 MAX = mybir.AluOpType.max
+AND = mybir.AluOpType.bitwise_and
 EXP = mybir.ActivationFunctionType.Exp
 COPY = mybir.ActivationFunctionType.Copy
 AX_X = mybir.AxisListType.X
@@ -30,10 +31,8 @@ C_LO = LN_ALPHA - C_HI
 FLOPS = 2 * 2 * BH * S * S * D
 
 LA = 3
-XMODE = "g"
 PIN = True
 PEMASK = tuple(range(2, 62, 5))
-TAILS = 1
 
 
 def tile_dotproductattention_t_kernel(tc, q, k, v, attn_mask, out):
@@ -54,10 +53,18 @@ def tile_dotproductattention_t_kernel(tc, q, k, v, attn_mask, out):
         identb = const.tile([P, P], BF16)
         make_identity(nc, identb[:])
 
-        j_i = const.tile([P, NT], I32)
-        nc.gpsimd.iota(j_i[:], pattern=[[1, NT]], base=0, channel_multiplier=NT)
+        a_i = const.tile([P, NT], I32)
+        nc.gpsimd.iota(a_i[:], pattern=[[2, 2], [256, 2]], base=0, channel_multiplier=1)
+        b_i = const.tile([P, NT], I32)
+        nc.gpsimd.iota(b_i[:], pattern=[[0, NT]], base=0, channel_multiplier=1)
+        c_i = const.tile([P, NT], I32)
+        nc.vector.tensor_scalar(out=c_i[:], in0=b_i[:], scalar1=126, scalar2=None, op0=AND)
+        a_f = const.tile([P, NT], F32)
+        nc.vector.tensor_copy(out=a_f[:], in_=a_i[:])
+        c_f = const.tile([P, NT], F32)
+        nc.vector.tensor_copy(out=c_f[:], in_=c_i[:])
         j_f = const.tile([P, NT], F32)
-        nc.vector.tensor_copy(out=j_f[:], in_=j_i[:])
+        nc.vector.tensor_tensor(out=j_f[:], in0=a_f[:], in1=c_f[:], op=ADD)
         n_f = const.tile([P, NT], F32)
         nc.vector.tensor_scalar(out=n_f[:], in0=j_f[:], scalar1=-1.0, scalar2=float(S - 1), op0=MULT, op1=ADD)
         grow = const.tile([P, NT], F32)
@@ -105,23 +112,27 @@ def tile_dotproductattention_t_kernel(tc, q, k, v, attn_mask, out):
             nc.scalar.copy(out=qT[:], in_=hd[h]["qps"][:])
             hd[h]["qTb"] = qT[:].bitcast(BF16).rearrange("w (t p e) -> w t p e", t=NT, e=2)
 
+        def upe(ap):
+            return ap.rearrange("w (u p e) -> w u p e", u=2, e=2)
+
         def xk(h):
             if h < 0 or h >= BH:
                 return
             kT = wk.tile([P, S], F32, tag="kT", name="kT", bufs=2)
             if h == 0:
-                nc.vector.tensor_copy(out=kT[:], in_=hd[h]["kps"][:])
+                nc.vector.tensor_copy(out=upe(kT[:]), in_=hd[h]["kps"][:].rearrange("w (u e p) -> w u p e", u=2, e=2))
             else:
-                nc.scalar.copy(out=kT[:], in_=hd[h]["kps"][:])
+                nc.scalar.copy(out=upe(kT[:]), in_=hd[h]["kps"][:].rearrange("w (u e p) -> w u p e", u=2, e=2))
             hd[h]["kTb"] = kT[:].bitcast(BF16).rearrange("w (j e) -> w j e", e=2)
 
         def rgv(h):
             if h < 0 or h >= BH:
                 return
             vg = wk.tile([P, D * NT], BF16, tag="vg", name="vg", align_bytes=64, bufs=2)
-            nc.vector.tensor_copy(
-                out=vg[:].rearrange("p (c i t) -> p c t i", i=4, t=NT),
-                in_=hd[h]["v"][:].rearrange("p (t c i) -> p c t i", t=NT, i=4),
+            nc.gpsimd.tensor_scalar(
+                out=vg[:].rearrange("p (d t) -> p d t", t=NT),
+                in0=hd[h]["v"][:].rearrange("p (t d) -> p d t", t=NT),
+                scalar1=1.0, scalar2=0.0, op0=MULT, op1=ADD,
             )
             hd[h]["vg"] = vg
 
@@ -136,10 +147,7 @@ def tile_dotproductattention_t_kernel(tc, q, k, v, attn_mask, out):
 
         def mview(kk):
             t = kk % NT
-            return hd[kk // NT]["m"][:, t * S:(t + 1) * S].rearrange("i (p c) -> i c p", c=NT)
-
-        def cview(ap):
-            return ap.rearrange("i (c p) -> i c p", c=NT)
+            return hd[kk // NT]["m"][:, t * S:(t + 1) * S].rearrange("i (p u e) -> i u p e", u=2, e=2)
 
         def mm(kq, e):
             if kq < 0 or kq >= NTILES:
@@ -152,7 +160,7 @@ def tile_dotproductattention_t_kernel(tc, q, k, v, attn_mask, out):
             s_ps = tl[kq]["s_ps"]
             nc.tensor.matmul(s_ps[:], lhsT=st["qTb"][:, t, :, e], rhs=st["kTb"][:, :, e], start=(e == 0), stop=False)
             if e == 1 and kq in PEMASK:
-                nc.tensor.matmul(cview(s_ps[:]), lhsT=identb[:], rhs=mview(kq), start=False, stop=False)
+                nc.tensor.matmul(upe(s_ps[:]), lhsT=identb[:], rhs=mview(kq), start=False, stop=False)
 
         def dec(kq, cs):
             if kq < 0 or kq >= NTILES:
@@ -168,16 +176,16 @@ def tile_dotproductattention_t_kernel(tc, q, k, v, attn_mask, out):
                     is_transpose=True,
                 )
 
-        def etr(ke, cs):
+        def etr(ke, u):
             if ke < 0 or ke >= NTILES:
                 return
             n = ke // 2
             a = ke % 2
-            if a == 0 and cs[0] == 0:
-                eT_new = ps_et.tile([P, 2, NT, P], BF16, tag="et", name="eT_ps")
+            if a == 0 and u == 0:
+                eT_new = ps_et.tile([P, 2, 2, P], F32, tag="et", name="eT_ps")
                 pr[n]["eT_ps"] = eT_new
-            for c in cs:
-                nc.tensor.transpose(pr[n]["eT_ps"][:, a, c, :], tl[ke]["e_sb"][:, c * P:(c + 1) * P], identb[:])
+            words = tl[ke]["e_sb"][:].bitcast(F32)
+            nc.tensor.transpose(pr[n]["eT_ps"][:, a, u, :], words[:, u * P:(u + 1) * P], ident32[:])
 
         def badd(kk):
             if kk < 0 or kk >= NTILES:
@@ -186,7 +194,7 @@ def tile_dotproductattention_t_kernel(tc, q, k, v, attn_mask, out):
                 tl[kk]["s_src"] = tl[kk]["s_ps"]
             else:
                 s_sb = wk.tile([P, S], F32, tag="s_sb", name="s_sb", bufs=5)
-                nc.vector.tensor_tensor(out=cview(s_sb[:]), in0=cview(tl[kk]["s_ps"][:]), in1=mview(kk), op=ADD)
+                nc.vector.tensor_tensor(out=upe(s_sb[:]), in0=upe(tl[kk]["s_ps"][:]), in1=mview(kk), op=ADD)
                 tl[kk]["s_src"] = s_sb
 
         def cmax(kk):
@@ -214,20 +222,11 @@ def tile_dotproductattention_t_kernel(tc, q, k, v, attn_mask, out):
         def xe(n):
             if n < 0 or n >= NPAIRS:
                 return
-            grp = wk.tile([P, 2 * P * NT], BF16, tag="grp", name="grp", align_bytes=64, bufs=1)
-            if XMODE == "g" and n < NPAIRS - TAILS:
-                etc = wk.tile([P, 2 * NT * P], BF16, tag="etc", name="etc", bufs=3)
-                nc.scalar.copy(out=etc[:], in_=pr[n]["eT_ps"][:].rearrange("p a c i -> p (a c i)"))
-                nc.gpsimd.tensor_scalar(
-                    out=grp[:].rearrange("p (a i c) -> p a i c", a=2, c=NT),
-                    in0=etc[:].rearrange("p (a c i) -> p a i c", a=2, c=NT),
-                    scalar1=1.0, scalar2=0.0, op0=MULT, op1=ADD,
-                )
-            else:
-                nc.scalar.copy(
-                    out=grp[:].rearrange("p (a i c) -> p a i c", a=2, c=NT),
-                    in_=pr[n]["eT_ps"][:].rearrange("p a c i -> p a i c"),
-                )
+            grp = wk.tile([P, 2 * P * NT], BF16, tag="grp", name="grp", align_bytes=64, bufs=2)
+            nc.scalar.copy(
+                out=grp[:].bitcast(F32).rearrange("p (a i u) -> p a i u", a=2, u=2),
+                in_=pr[n]["eT_ps"][:].rearrange("p a u i -> p a i u"),
+            )
             pr[n]["grp"] = grp
 
         def qe(n):
@@ -297,26 +296,28 @@ def tile_dotproductattention_t_kernel(tc, q, k, v, attn_mask, out):
         for s in range(-8, NTILES + 13):
             if s >= 0 and s % 4 == 0:
                 load(s // 4 + LA)
-            if (s - 11) % 4 == 0 and (s - 11) // 4 < BH - 1:
-                store((s - 11) // 4)
-            if s == NTILES + 5:
+            if (s - 10) % 4 == 0 and (s - 10) // 4 < BH - 1:
+                store((s - 10) // 4)
+            if s == NTILES + 4:
                 store_half(BH - 1, 0)
-            if s == NTILES + 7:
+            if s == NTILES + 6:
                 store_half(BH - 1, 1)
             mm(s + 3, 0)
             dec(s + 2, (0, 1))
-            etr(s - 2, (0, 1))
+            etr(s - 2, 0)
             mm(s + 3, 1)
             dec(s + 2, (2, 3))
-            etr(s - 2, (2, 3))
+            etr(s - 2, 1)
             if (s + 8) % 4 == 0:
                 tqk((s + 8) // 4, "q")
             if s == -8:
                 tqk(0, "k")
             if (s + 6) % 4 == 0 and s > -6:
                 tqk((s + 6) // 4, "k")
-            if (s - 7) % 2 == 0:
-                pv((s - 7) // 2)
+            if (s - 6) % 2 == 0:
+                pv((s - 6) // 2)
+            if s % 4 == 0:
+                rgv(s // 4)
             if s == -7:
                 xk(0)
             if s + 1 in PEMASK:
@@ -326,21 +327,19 @@ def tile_dotproductattention_t_kernel(tc, q, k, v, attn_mask, out):
                 badd(s + 1)
             if s not in PEMASK:
                 cmax(s)
-            if (s - 2) % 4 == 0:
-                rgv((s - 2) // 4)
             if (s - 4) % 4 == 0:
                 qv((s - 4) // 4)
-            if (s - 6) % 2 == 0:
-                qe((s - 6) // 2)
+            if (s - 5) % 2 == 0:
+                qe((s - 5) // 2)
             if s in PEMASK:
                 dexp(s)
             if s - 1 not in PEMASK:
                 dexp(s - 1)
             if (s - 4) % 2 == 0:
                 xe((s - 4) // 2)
-            if (s - 8) % 2 == 0:
-                oex(s - 8)
+            if (s - 7) % 2 == 0:
                 oex(s - 7)
+                oex(s - 6)
             if (s + 7) % 4 == 0:
                 xq((s + 7) // 4)
             if (s + 5) % 4 == 0 and s > -5:

@@ -75,6 +75,9 @@ def tile_dotproductattention_t_kernel(tc, q, k, v, attn_mask, out):
         nc.vector.scalar_tensor_tensor(out=low2[:], in0=grow[:], scalar=EPS, in1=low[:], op0=MULT, op1=ADD)
         dcol = const.tile([P, NT], F32)
         nc.vector.scalar_tensor_tensor(out=dcol[:], in0=n_f[:], scalar=C_HI, in1=low2[:], op0=MULT, op1=ADD)
+        dmat = const.tile([P, S], F32)
+        for c in range(NT):
+            nc.vector.tensor_copy(out=dmat[:, c * P:(c + 1) * P], in_=dcol[:, c:c + 1].to_broadcast([P, P]))
 
         hd = {}
         pr = {}
@@ -169,7 +172,7 @@ def tile_dotproductattention_t_kernel(tc, q, k, v, attn_mask, out):
             for c in cs:
                 nc.tensor.matmul(
                     s_ps[:, c * P:(c + 1) * P],
-                    lhsT=dcol[:, c:c + 1].to_broadcast([P, P]),
+                    lhsT=dmat[:, c * P:(c + 1) * P],
                     rhs=ident32[:],
                     start=False,
                     stop=(c == NT - 1),

@@ -32,7 +32,7 @@ FLOPS = 2 * 2 * BH * S * S * D
 
 LA = 3
 PIN = True
-PEMASK = tuple(range(2, 62, 5))
+PEMASK = tuple(kk for kk in range(NTILES) if kk % 4 == 2 and kk % 16 != 14)
 
 
 def tile_dotproductattention_t_kernel(tc, q, k, v, attn_mask, out):
@@ -42,9 +42,9 @@ def tile_dotproductattention_t_kernel(tc, q, k, v, attn_mask, out):
         ld = ctx.enter_context(tc.tile_pool(name="ld", bufs=LA + 1))
         wk = ctx.enter_context(tc.tile_pool(name="wk", bufs=2))
         ps_tr = ctx.enter_context(tc.psum_pool(name="ps_tr", bufs=1))
-        ps_s = ctx.enter_context(tc.psum_pool(name="ps_s", bufs=4))
+        ps_s = ctx.enter_context(tc.psum_pool(name="ps_s", bufs=3))
         ps_et = ctx.enter_context(tc.psum_pool(name="ps_et", bufs=2))
-        ps_o = ctx.enter_context(tc.psum_pool(name="ps_o", bufs=1))
+        ps_o = ctx.enter_context(tc.psum_pool(name="ps_o", bufs=2))
         if PIN:
             ctx.enter_context(tc.manual_schedule())
 
@@ -82,51 +82,89 @@ def tile_dotproductattention_t_kernel(tc, q, k, v, attn_mask, out):
         hd = {}
         pr = {}
         tl = {}
+        groups = [(kk, kk + 1) for kk in range(0, NTILES - 2, 2)] + [(NTILES - 2,), (NTILES - 1,)]
+        XE = {g: g[-1] + 3 for g in groups}
+        QE = {g: g[-1] + 4 for g in groups}
+        PV = {g: g[-1] + (6 if len(g) == 2 else 5) for g in groups}
+        OEX = {kk: PV[g] + 1 + a for g in groups for a, kk in enumerate(g)}
 
-        def load(h):
+        def gof(kk):
+            g = groups[min(kk // 2, NTILES // 2 - 1)] if kk < NTILES - 1 else groups[-1]
+            return g, kk - g[0]
+
+        def at(s, when):
+            return [x for x in when if when[x] == s]
+
+        def load(h, which):
             if h < 0 or h >= BH:
                 return
-            q_sb = ld.tile([P, NT * D], BF16, tag="q", name="q_sb")
-            nc.sync.dma_start(out=q_sb[:], in_=q[h].rearrange("(p t) d -> p (t d)", t=NT))
-            k_sb = ld.tile([P, NT * D], BF16, tag="k", name="k_sb")
-            nc.sync.dma_start(out=k_sb[:], in_=k[h].rearrange("(p t) d -> p (t d)", t=NT))
-            m_sb = ld.tile([P, NT * S], BF16, tag="m", name="m_sb")
-            nc.sync.dma_start(out=m_sb[:], in_=attn_mask[h].rearrange("(p t) j -> p (t j)", t=NT))
-            v_sb = ld.tile([P, NT * D], BF16, tag="v", name="v_sb")
-            nc.sync.dma_start(out=v_sb[:], in_=v[h].rearrange("(p t) d -> p (t d)", t=NT))
-            hd[h] = {"q": q_sb, "k": k_sb, "m": m_sb, "v": v_sb}
+            if h not in hd:
+                hd[h] = {}
+            cols = NT * S if which == "m" else NT * D
+            x_sb = ld.tile([P, cols], BF16, tag=which, name="x_sb")
+            src = {"q": q, "k": k, "m": attn_mask, "v": v}[which][h].rearrange("(p t) d -> p (t d)", t=NT)
+            cuts = (0, S, cols) if h == 0 and which == "m" else (0, cols)
+            for a, b in zip(cuts[:-1], cuts[1:]):
+                nc.sync.dma_start(out=x_sb[:, a:b], in_=src[:, a:b])
+            hd[h][which] = x_sb
 
         def tqk(h, which):
             if h < 0 or h >= BH:
                 return
             src = hd[h][which][:].bitcast(F32)
-            if h == 0 and which == "k":
-                t_ps = ps_o.tile([P, S], F32, tag="o", name="t_ps0")
-            else:
-                t_ps = ps_tr.tile([P, S], F32, tag="tr", name="t_ps")
+            t_ps = ps_tr.tile([P, S], F32, tag="tr", name="t_ps")
             for t in range(NT):
                 nc.tensor.transpose(t_ps[:, t * P:(t + 1) * P], src[:, t * P:(t + 1) * P], ident32[:])
             hd[h][which + "ps"] = t_ps
 
-        def xq(h):
-            if h < 0 or h >= BH:
-                return
-            qT = wk.tile([P, S], F32, tag="qT", name="qT", bufs=2)
-            nc.scalar.copy(out=qT[:], in_=hd[h]["qps"][:])
-            hd[h]["qTb"] = qT[:].bitcast(BF16).rearrange("w (t p e) -> w t p e", t=NT, e=2)
-
         def upe(ap):
             return ap.rearrange("w (u p e) -> w u p e", u=2, e=2)
 
-        def xk(h):
-            if h < 0 or h >= BH:
-                return
+        def newq(h):
+            qT = wk.tile([P, S], F32, tag="qT", name="qT", bufs=2)
+            hd[h]["qTb"] = qT[:].bitcast(BF16).rearrange("w (t p e) -> w t p e", t=NT, e=2)
+            return qT
+
+        def newk(h):
             kT = wk.tile([P, S], F32, tag="kT", name="kT", bufs=2)
-            if h == 0:
-                nc.vector.tensor_copy(out=upe(kT[:]), in_=hd[h]["kps"][:].rearrange("w (u e p) -> w u p e", u=2, e=2))
-            else:
-                nc.scalar.copy(out=upe(kT[:]), in_=hd[h]["kps"][:].rearrange("w (u e p) -> w u p e", u=2, e=2))
             hd[h]["kTb"] = kT[:].bitcast(BF16).rearrange("w (j e) -> w j e", e=2)
+            return kT
+
+        def first_qk():
+            ksrc = hd[0]["k"][:].bitcast(F32)
+            qsrc = hd[0]["q"][:].bitcast(F32)
+            ka = ps_tr.tile([P, S], F32, tag="tr", name="ka")
+            kb = ps_o.tile([P, S], F32, tag="o", name="kb")
+            qa = ps_o.tile([P, S], F32, tag="o", name="qa")
+            for t in range(2):
+                nc.tensor.transpose(ka[:, t * P:(t + 1) * P], ksrc[:, t * P:(t + 1) * P], ident32[:])
+            for t in range(2):
+                nc.tensor.transpose(kb[:, t * P:(t + 1) * P], ksrc[:, (t + 2) * P:(t + 3) * P], ident32[:])
+            for t in range(NT):
+                nc.tensor.transpose(qa[:, t * P:(t + 1) * P], qsrc[:, t * P:(t + 1) * P], ident32[:])
+            kT = newk(0)
+            qT = newq(0)
+            H = S // 2
+            nc.vector.tensor_copy(
+                out=kT[:, 0:H].rearrange("w (p e) -> w p e", e=2), in_=ka[:, 0:H].rearrange("w (e p) -> w p e", e=2)
+            )
+            nc.scalar.copy(
+                out=kT[:, H:S].rearrange("w (p e) -> w p e", e=2), in_=kb[:, 0:H].rearrange("w (e p) -> w p e", e=2)
+            )
+            nc.vector.tensor_copy(out=qT[:, 0:P], in_=qa[:, 0:P])
+            nc.scalar.copy(out=qT[:, P:S], in_=qa[:, P:S])
+
+        def xq(h):
+            if h < 1 or h >= BH:
+                return
+            qT = newq(h)
+            nc.scalar.copy(out=qT[:], in_=hd[h]["qps"][:])
+
+        def xk(h):
+            if h < 1 or h >= BH:
+                return
+            kT = newk(h)
+            nc.scalar.copy(out=upe(kT[:]), in_=hd[h]["kps"][:].rearrange("w (u e p) -> w u p e", u=2, e=2))
 
         def rgv(h):
             if h < 0 or h >= BH:
@@ -179,16 +217,19 @@ def tile_dotproductattention_t_kernel(tc, q, k, v, attn_mask, out):
                     is_transpose=True,
                 )
 
-        def etr(ke, u):
+        def etr(ke):
             if ke < 0 or ke >= NTILES:
                 return
-            n = ke // 2
-            a = ke % 2
-            if a == 0 and u == 0:
-                eT_new = ps_et.tile([P, 2, 2, P], F32, tag="et", name="eT_ps")
-                pr[n]["eT_ps"] = eT_new
+            g, a = gof(ke)
+            if a == 0:
+                if ke == NTILES - 1:
+                    eT_new = ps_s.tile([P, 1, 2, P], F32, tag="s", name="eT_ps")
+                else:
+                    eT_new = ps_et.tile([P, len(g), 2, P], F32, tag="et", name="eT_ps")
+                pr[g]["eT_ps"] = eT_new
             words = tl[ke]["e_sb"][:].bitcast(F32)
-            nc.tensor.transpose(pr[n]["eT_ps"][:, a, u, :], words[:, u * P:(u + 1) * P], ident32[:])
+            for u in range(2):
+                nc.tensor.transpose(pr[g]["eT_ps"][:, a, u, :], words[:, u * P:(u + 1) * P], ident32[:])
 
         def badd(kk):
             if kk < 0 or kk >= NTILES:
@@ -210,119 +251,113 @@ def tile_dotproductattention_t_kernel(tc, q, k, v, attn_mask, out):
         def dexp(kk):
             if kk < 0 or kk >= NTILES:
                 return
-            n = kk // 2
-            a = kk % 2
-            if n not in pr:
-                rsum_new = wk.tile([P, 2], F32, tag="rsum", name="rsum", bufs=6)
-                pr[n] = {"rsum": rsum_new}
+            g, a = gof(kk)
+            if a == 0:
+                rsum_new = wk.tile([P, len(g)], F32, tag="rsum", name="rsum", bufs=6)
+                pr[g] = {"rsum": rsum_new}
             e_sb = wk.tile([P, S], BF16, tag="e_sb", name="e_sb", bufs=4)
             nc.scalar.activation(
                 out=e_sb[:], in_=tl[kk]["s_src"][:], func=EXP, bias=tl[kk]["negm"][:], scale=1.0,
-                accum_out=pr[n]["rsum"][:, a:a + 1],
+                accum_out=pr[g]["rsum"][:, a:a + 1],
             )
             tl[kk]["e_sb"] = e_sb
 
-        def xe(n):
-            if n < 0 or n >= NPAIRS:
-                return
-            grp = wk.tile([P, 2 * P * NT], BF16, tag="grp", name="grp", align_bytes=64, bufs=2)
+        def xe(g):
+            w = len(g)
+            grp = wk.tile([P, w * P * NT], BF16, tag="grp%d" % w, name="grp", align_bytes=64, bufs=2)
             nc.scalar.copy(
-                out=grp[:].bitcast(F32).rearrange("p (a i u) -> p a i u", a=2, u=2),
-                in_=pr[n]["eT_ps"][:].rearrange("p a u i -> p a i u"),
+                out=grp[:].bitcast(F32).rearrange("p (a i u) -> p a i u", a=w, u=2),
+                in_=pr[g]["eT_ps"][:].rearrange("p a u i -> p a i u"),
             )
-            pr[n]["grp"] = grp
+            pr[g]["grp"] = grp
 
-        def qe(n):
-            if n < 0 or n >= NPAIRS:
-                return
-            ecod = wk.tile([P, 2 * P], U32, tag="ecod", name="ecod", align_bytes=64, bufs=3)
-            escl = wk.tile([P, 2 * P], U8, tag="escl", name="escl", align_bytes=64, bufs=3)
-            nc.vector.quantize_mx(out=ecod[:].bitcast(FP8X4), scales=escl[:], in_=pr[n]["grp"][:])
-            rinv = wk.tile([P, 2], F32, tag="rinv", name="rinv", bufs=4)
-            nc.vector.reciprocal(rinv[:], pr[n]["rsum"][:])
-            pr[n]["ecod"] = ecod
-            pr[n]["escl"] = escl
-            pr[n]["rinv"] = rinv
+        def qe(g):
+            w = len(g)
+            ecod = wk.tile([P, w * P], U32, tag="ecod%d" % w, name="ecod", align_bytes=64, bufs=3)
+            escl = wk.tile([P, w * P], U8, tag="escl%d" % w, name="escl", align_bytes=64, bufs=3)
+            nc.vector.quantize_mx(out=ecod[:].bitcast(FP8X4), scales=escl[:], in_=pr[g]["grp"][:])
+            rinv = wk.tile([P, w], F32, tag="rinv", name="rinv", bufs=4)
+            nc.vector.reciprocal(rinv[:], pr[g]["rsum"][:])
+            pr[g]["ecod"] = ecod
+            pr[g]["escl"] = escl
+            pr[g]["rinv"] = rinv
 
-        def pv(n):
-            if n < 0 or n >= NPAIRS:
-                return
-            st = hd[n // 2]
-            o_ps = ps_o.tile([P, 2, D], F32, tag="o", name="o_ps")
-            for a in range(2):
+        def pv(g):
+            w = len(g)
+            st = hd[g[0] // NT]
+            if g[0] >= NTILES - 4:
+                o_ps = ps_s.tile([P, w, D], F32, tag="s", name="o_ps")
+            else:
+                o_ps = ps_o.tile([P, w, D], F32, tag="o", name="o_ps")
+            for a in range(w):
                 nc.tensor.matmul_mx(
                     out=o_ps[:, a, :],
-                    lhsT=pr[n]["ecod"][:, a * P:(a + 1) * P].bitcast(FP8X4),
-                    lhsT_scale=pr[n]["escl"][:, a * P:(a + 1) * P],
+                    lhsT=pr[g]["ecod"][:, a * P:(a + 1) * P].bitcast(FP8X4),
+                    lhsT_scale=pr[g]["escl"][:, a * P:(a + 1) * P],
                     rhs=st["vcod"][:].bitcast(FP8X4),
                     rhs_scale=st["vscl"][:],
                     start=True,
                     stop=True,
                 )
-            pr[n]["o_ps"] = o_ps
+            pr[g]["o_ps"] = o_ps
+
+        def on_vector(kk):
+            return kk % 4 == 2 or (kk >= NTILES - 8 and kk % 2 == 0)
 
         def oex(kk):
-            if kk < 0 or kk >= NTILES:
-                return
             h = kk // NT
             t = kk % NT
-            n = kk // 2
-            a = kk % 2
+            g, a = gof(kk)
             if t == 0:
                 o_new = wk.tile([P, NT * D], F32, tag="o_sb", name="o_sb", bufs=3)
                 hd[h]["o_sb"] = o_new
             o_sb = hd[h]["o_sb"]
-            if n % 4 == 3:
+            if on_vector(kk):
                 nc.vector.tensor_scalar(
-                    out=o_sb[:, t * D:(t + 1) * D], in0=pr[n]["o_ps"][:, a, :], scalar1=pr[n]["rinv"][:, a:a + 1],
+                    out=o_sb[:, t * D:(t + 1) * D], in0=pr[g]["o_ps"][:, a, :], scalar1=pr[g]["rinv"][:, a:a + 1],
                     scalar2=None, op0=MULT,
                 )
             else:
                 nc.scalar.activation(
-                    out=o_sb[:, t * D:(t + 1) * D], in_=pr[n]["o_ps"][:, a, :], func=COPY,
-                    scale=pr[n]["rinv"][:, a:a + 1],
+                    out=o_sb[:, t * D:(t + 1) * D], in_=pr[g]["o_ps"][:, a, :], func=COPY,
+                    scale=pr[g]["rinv"][:, a:a + 1],
                 )
 
-        def store(h):
-            if h < 0 or h >= BH:
-                return
-            nc.sync.dma_start(out=out[h].rearrange("(p t) d -> p (t d)", t=NT), in_=hd[h]["o_sb"][:])
-
-        def store_half(h, half):
+        def store(h, a, b):
             nc.sync.dma_start(
-                out=out[h].rearrange("(p t) d -> p (t d)", t=NT)[:, half * 2 * D:(half + 1) * 2 * D],
-                in_=hd[h]["o_sb"][:, half * 2 * D:(half + 1) * 2 * D],
+                out=out[h].rearrange("(p t) d -> p (t d)", t=NT)[:, a * D:b * D], in_=hd[h]["o_sb"][:, a * D:b * D]
             )
 
-        for h in range(LA):
-            load(h)
-        for s in range(-8, NTILES + 13):
+        for h, which in ((0, "k"), (0, "q"), (0, "m"), (1, "q"), (1, "k"), (0, "v"), (1, "m"), (1, "v")):
+            load(h, which)
+        for which in ("q", "k", "m", "v"):
+            load(2, which)
+        first_qk()
+        for s in range(-3, NTILES + 9):
             if s >= 0 and s % 4 == 0:
-                load(s // 4 + LA)
-            if (s - 10) % 4 == 0 and (s - 10) // 4 < BH - 1:
-                store((s - 10) // 4)
-            if s == NTILES + 4:
-                store_half(BH - 1, 0)
-            if s == NTILES + 6:
-                store_half(BH - 1, 1)
-            mm(s + 3, 0)
-            dec(s + 2, (0, 1))
-            etr(s - 2, 0)
-            mm(s + 3, 1)
-            dec(s + 2, (2, 3))
-            etr(s - 2, 1)
-            if (s + 8) % 4 == 0:
-                tqk((s + 8) // 4, "q")
-            if s == -8:
-                tqk(0, "k")
-            if (s + 6) % 4 == 0 and s > -6:
-                tqk((s + 6) // 4, "k")
-            if (s - 6) % 2 == 0:
-                pv((s - 6) // 2)
+                for which in ("q", "k", "m", "v"):
+                    load(s // 4 + LA, which)
+            if (s - 12) % 4 == 0 and (s - 12) // 4 >= 0 and (s - 12) // 4 < BH - 1:
+                store((s - 12) // 4, 0, NT)
+            mm(s + 2, 0)
+            for g in at(s, PV):
+                pv(g)
+            mm(s + 2, 1)
+            dec(s + 2, range(NT))
+            etr(s - 2)
+            if s == -2:
+                tqk(1, "q")
+            if s == -1:
+                tqk(1, "k")
+            if s >= 0 and s % 4 == 0:
+                tqk(s // 4 + 2, "q")
+            if s >= 0 and s % 4 == 2:
+                tqk(s // 4 + 2, "k")
             if s % 4 == 0:
                 rgv(s // 4)
-            if s == -7:
-                xk(0)
+            for kk in at(s, OEX):
+                if on_vector(kk):
+                    oex(kk)
             if s + 1 in PEMASK:
                 badd(s + 1)
                 cmax(s + 1)
@@ -332,18 +367,25 @@ def tile_dotproductattention_t_kernel(tc, q, k, v, attn_mask, out):
                 cmax(s)
             if (s - 4) % 4 == 0:
                 qv((s - 4) // 4)
-            if (s - 5) % 2 == 0:
-                qe((s - 5) // 2)
+            for g in at(s, QE):
+                qe(g)
+            for kk in at(s, OEX):
+                if not on_vector(kk):
+                    oex(kk)
             if s in PEMASK:
                 dexp(s)
             if s - 1 not in PEMASK:
                 dexp(s - 1)
-            if (s - 4) % 2 == 0:
-                xe((s - 4) // 2)
-            if (s - 7) % 2 == 0:
-                oex(s - 7)
-                oex(s - 6)
-            if (s + 7) % 4 == 0:
-                xq((s + 7) // 4)
-            if (s + 5) % 4 == 0 and s > -5:
-                xk((s + 5) // 4)
+            for g in at(s, XE):
+                xe(g)
+            if s == -1:
+                xq(1)
+            if s == 0:
+                xk(1)
+            if s >= 0 and s % 4 == 1:
+                xq(s // 4 + 2)
+            if s >= 0 and s % 4 == 3:
+                xk(s // 4 + 2)
+            for kk in at(s, OEX):
+                if kk >= NTILES - NT:
+                    store(BH - 1, kk % NT, kk % NT + 1)

@@ -42,9 +42,9 @@ def tile_dotproductattention_t_kernel(tc, q, k, v, attn_mask, out):
         ld = ctx.enter_context(tc.tile_pool(name="ld", bufs=LA + 1))
         wk = ctx.enter_context(tc.tile_pool(name="wk", bufs=2))
         ps_tr = ctx.enter_context(tc.psum_pool(name="ps_tr", bufs=1))
-        ps_s = ctx.enter_context(tc.psum_pool(name="ps_s", bufs=3))
+        ps_s = ctx.enter_context(tc.psum_pool(name="ps_s", bufs=4))
         ps_et = ctx.enter_context(tc.psum_pool(name="ps_et", bufs=2))
-        ps_o = ctx.enter_context(tc.psum_pool(name="ps_o", bufs=2))
+        ps_o = ctx.enter_context(tc.psum_pool(name="ps_o", bufs=1))
         if PIN:
             ctx.enter_context(tc.manual_schedule())
 
@@ -135,7 +135,7 @@ def tile_dotproductattention_t_kernel(tc, q, k, v, attn_mask, out):
             qsrc = hd[0]["q"][:].bitcast(F32)
             ka = ps_tr.tile([P, S], F32, tag="tr", name="ka")
             kb = ps_o.tile([P, S], F32, tag="o", name="kb")
-            qa = ps_o.tile([P, S], F32, tag="o", name="qa")
+            qa = ps_et.tile([P, S], F32, tag="et", name="qa")
             for t in range(2):
                 nc.tensor.transpose(ka[:, t * P:(t + 1) * P], ksrc[:, t * P:(t + 1) * P], ident32[:])
             for t in range(2):
@@ -217,19 +217,18 @@ def tile_dotproductattention_t_kernel(tc, q, k, v, attn_mask, out):
                     is_transpose=True,
                 )
 
-        def etr(ke):
+        def etr(ke, u):
             if ke < 0 or ke >= NTILES:
                 return
             g, a = gof(ke)
-            if a == 0:
+            if a == 0 and u == 0:
                 if ke == NTILES - 1:
                     eT_new = ps_s.tile([P, 1, 2, P], F32, tag="s", name="eT_ps")
                 else:
                     eT_new = ps_et.tile([P, len(g), 2, P], F32, tag="et", name="eT_ps")
                 pr[g]["eT_ps"] = eT_new
             words = tl[ke]["e_sb"][:].bitcast(F32)
-            for u in range(2):
-                nc.tensor.transpose(pr[g]["eT_ps"][:, a, u, :], words[:, u * P:(u + 1) * P], ident32[:])
+            nc.tensor.transpose(pr[g]["eT_ps"][:, a, u, :], words[:, u * P:(u + 1) * P], ident32[:])
 
         def badd(kk):
             if kk < 0 or kk >= NTILES:
@@ -339,12 +338,12 @@ def tile_dotproductattention_t_kernel(tc, q, k, v, attn_mask, out):
                     load(s // 4 + LA, which)
             if (s - 12) % 4 == 0 and (s - 12) // 4 >= 0 and (s - 12) // 4 < BH - 1:
                 store((s - 12) // 4, 0, NT)
-            mm(s + 2, 0)
-            for g in at(s, PV):
-                pv(g)
-            mm(s + 2, 1)
-            dec(s + 2, range(NT))
-            etr(s - 2)
+            mm(s + 3, 0)
+            dec(s + 2, (0, 1))
+            etr(s - 2, 0)
+            mm(s + 3, 1)
+            dec(s + 2, (2, 3))
+            etr(s - 2, 1)
             if s == -2:
                 tqk(1, "q")
             if s == -1:
@@ -353,6 +352,8 @@ def tile_dotproductattention_t_kernel(tc, q, k, v, attn_mask, out):
                 tqk(s // 4 + 2, "q")
             if s >= 0 and s % 4 == 2:
                 tqk(s // 4 + 2, "k")
+            for g in at(s, PV):
+                pv(g)
             if s % 4 == 0:
                 rgv(s // 4)
             for kk in at(s, OEX):

import math
from contextlib import ExitStack

import concourse.mybir as mybir
from concourse.masks import make_identity

F32 = mybir.dt.float32
BF16 = mybir.dt.bfloat16
I32 = mybir.dt.int32
U32 = mybir.dt.uint32
U8 = mybir.dt.uint8
FP8X4 = mybir.dt.float8_e4m3fn_x4
ADD = mybir.AluOpType.add
MULT = mybir.AluOpType.mult
MAX = mybir.AluOpType.max
AND = mybir.AluOpType.bitwise_and
EXP = mybir.ActivationFunctionType.Exp
COPY = mybir.ActivationFunctionType.Copy
AX_X = mybir.AxisListType.X

P = 128
BH, S, D = 16, 512, 256
NT = S // P
NTILES = BH * NT
NPAIRS = NTILES // 2
ALPHA = 0.99
EPS = 1e-10
LN_ALPHA = math.log(ALPHA)
C_HI = round(LN_ALPHA * 2097152.0) / 2097152.0
C_LO = LN_ALPHA - C_HI
FLOPS = 2 * 2 * BH * S * S * D

LA = 3
PIN = True
PEMASK = tuple(kk for kk in range(NTILES) if kk % 4 == 2 and kk % 16 != 14)


def tile_dotproductattention_t_kernel(tc, q, k, v, attn_mask, out):
    nc = tc.nc
    with ExitStack() as ctx:
        const = ctx.enter_context(tc.tile_pool(name="const", bufs=1))
        ld = ctx.enter_context(tc.tile_pool(name="ld", bufs=LA + 1))
        wk = ctx.enter_context(tc.tile_pool(name="wk", bufs=2))
        ps_tr = ctx.enter_context(tc.psum_pool(name="ps_tr", bufs=1))
        ps_s = ctx.enter_context(tc.psum_pool(name="ps_s", bufs=4))
        ps_et = ctx.enter_context(tc.psum_pool(name="ps_et", bufs=2))
        ps_o = ctx.enter_context(tc.psum_pool(name="ps_o", bufs=1))
        if PIN:
            ctx.enter_context(tc.manual_schedule())

        ident32 = const.tile([P, P], F32)
        make_identity(nc, ident32[:])
        identb = const.tile([P, P], BF16)
        make_identity(nc, identb[:])

        a_i = const.tile([P, NT], I32)
        nc.gpsimd.iota(a_i[:], pattern=[[2, 2], [256, 2]], base=0, channel_multiplier=1)
        b_i = const.tile([P, NT], I32)
        nc.gpsimd.iota(b_i[:], pattern=[[0, NT]], base=0, channel_multiplier=1)
        c_i = const.tile([P, NT], I32)
        nc.vector.tensor_scalar(out=c_i[:], in0=b_i[:], scalar1=126, scalar2=None, op0=AND)
        a_f = const.tile([P, NT], F32)
        nc.vector.tensor_copy(out=a_f[:], in_=a_i[:])
        c_f = const.tile([P, NT], F32)
        nc.vector.tensor_copy(out=c_f[:], in_=c_i[:])
        j_f = const.tile([P, NT], F32)
        nc.vector.tensor_tensor(out=j_f[:], in0=a_f[:], in1=c_f[:], op=ADD)
        n_f = const.tile([P, NT], F32)
        nc.vector.tensor_scalar(out=n_f[:], in0=j_f[:], scalar1=-1.0, scalar2=float(S - 1), op0=MULT, op1=ADD)
        grow = const.tile([P, NT], F32)
        nc.scalar.activation(out=grow[:], in_=n_f[:], func=EXP, scale=-LN_ALPHA)
        low = const.tile([P, NT], F32)
        nc.vector.tensor_scalar(out=low[:], in0=n_f[:], scalar1=C_LO, scalar2=None, op0=MULT)
        low2 = const.tile([P, NT], F32)
        nc.vector.scalar_tensor_tensor(out=low2[:], in0=grow[:], scalar=EPS, in1=low[:], op0=MULT, op1=ADD)
        dcol = const.tile([P, NT], F32)
        nc.vector.scalar_tensor_tensor(out=dcol[:], in0=n_f[:], scalar=C_HI, in1=low2[:], op0=MULT, op1=ADD)
        dmat = const.tile([P, S], F32)
        for c in range(NT):
            nc.vector.tensor_copy(out=dmat[:, c * P:(c + 1) * P], in_=dcol[:, c:c + 1].to_broadcast([P, P]))

        hd = {}
        pr = {}
        tl = {}
        groups = [(kk, kk + 1) for kk in range(0, NTILES - 2, 2)] + [(NTILES - 2,), (NTILES - 1,)]
        XE = {g: g[-1] + 3 for g in groups}
        QE = {g: g[-1] + 4 for g in groups}
        PV = {g: g[-1] + (6 if len(g) == 2 else 5) for g in groups}
        OEX = {kk: PV[g] + 1 + a for g in groups for a, kk in enumerate(g)}

        def gof(kk):
            g = groups[min(kk // 2, NTILES // 2 - 1)] if kk < NTILES - 1 else groups[-1]
            return g, kk - g[0]

        def at(s, when):
            return [x for x in when if when[x] == s]

        def load(h, which):
            if h < 0 or h >= BH:
                return
            if h not in hd:
                hd[h] = {}
            cols = NT * S if which == "m" else NT * D
            x_sb = ld.tile([P, cols], BF16, tag=which, name="x_sb")
            src = {"q": q, "k": k, "m": attn_mask, "v": v}[which][h].rearrange("(p t) d -> p (t d)", t=NT)
            cuts = (0, S, cols) if h == 0 and which == "m" else (0, cols)
            for a, b in zip(cuts[:-1], cuts[1:]):
                nc.sync.dma_start(out=x_sb[:, a:b], in_=src[:, a:b])
            hd[h][which] = x_sb

        def tqk(h, which):
            if h < 0 or h >= BH:
                return
            src = hd[h][which][:].bitcast(F32)
            t_ps = ps_tr.tile([P, S], F32, tag="tr", name="t_ps")
            for t in range(NT):
                nc.tensor.transpose(t_ps[:, t * P:(t + 1) * P], src[:, t * P:(t + 1) * P], ident32[:])
            hd[h][which + "ps"] = t_ps

        def upe(ap):
            return ap.rearrange("w (u p e) -> w u p e", u=2, e=2)

        def newq(h):
            qT = wk.tile([P, S], F32, tag="qT", name="qT", bufs=2)
            hd[h]["qTb"] = qT[:].bitcast(BF16).rearrange("w (t p e) -> w t p e", t=NT, e=2)
            return qT

        def newk(h):
            kT = wk.tile([P, S], F32, tag="kT", name="kT", bufs=2)
            hd[h]["kTb"] = kT[:].bitcast(BF16).rearrange("w (j e) -> w j e", e=2)
            return kT

        def first_qk():
            ksrc = hd[0]["k"][:].bitcast(F32)
            qsrc = hd[0]["q"][:].bitcast(F32)
            ka = ps_tr.tile([P, S], F32, tag="tr", name="ka")
            kb = ps_o.tile([P, S], F32, tag="o", name="kb")
            qa = ps_et.tile([P, S], F32, tag="et", name="qa")
            for t in range(2):
                nc.tensor.transpose(ka[:, t * P:(t + 1) * P], ksrc[:, t * P:(t + 1) * P], ident32[:])
            for t in range(2):
                nc.tensor.transpose(kb[:, t * P:(t + 1) * P], ksrc[:, (t + 2) * P:(t + 3) * P], ident32[:])
            for t in range(NT):
                nc.tensor.transpose(qa[:, t * P:(t + 1) * P], qsrc[:, t * P:(t + 1) * P], ident32[:])
            kT = newk(0)
            qT = newq(0)
            H = S // 2
            nc.vector.tensor_copy(
                out=kT[:, 0:H].rearrange("w (p e) -> w p e", e=2), in_=ka[:, 0:H].rearrange("w (e p) -> w p e", e=2)
            )
            nc.scalar.copy(
                out=kT[:, H:S].rearrange("w (p e) -> w p e", e=2), in_=kb[:, 0:H].rearrange("w (e p) -> w p e", e=2)
            )
            nc.vector.tensor_copy(out=qT[:, 0:P], in_=qa[:, 0:P])
            nc.scalar.copy(out=qT[:, P:S], in_=qa[:, P:S])

        def xq(h):
            if h < 1 or h >= BH:
                return
            qT = newq(h)
            nc.scalar.copy(out=qT[:], in_=hd[h]["qps"][:])

        def xk(h):
            if h < 1 or h >= BH:
                return
            kT = newk(h)
            nc.scalar.copy(out=upe(kT[:]), in_=hd[h]["kps"][:].rearrange("w (u e p) -> w u p e", u=2, e=2))

        def rgv(h):
            if h < 0 or h >= BH:
                return
            vg = wk.tile([P, D * NT], BF16, tag="vg", name="vg", align_bytes=64, bufs=2)
            nc.gpsimd.tensor_scalar(
                out=vg[:].rearrange("p (d t) -> p d t", t=NT),
                in0=hd[h]["v"][:].rearrange("p (t d) -> p d t", t=NT),
                scalar1=1.0, scalar2=0.0, op0=MULT, op1=ADD,
            )
            hd[h]["vg"] = vg

        def qv(h):
            if h < 0 or h >= BH:
                return
            vcod = wk.tile([P, D], U32, tag="vcod", name="vcod", align_bytes=64, bufs=3)
            vscl = wk.tile([P, D], U8, tag="vscl", name="vscl", align_bytes=64, bufs=3)
            nc.vector.quantize_mx(out=vcod[:].bitcast(FP8X4), scales=vscl[:], in_=hd[h]["vg"][:])
            hd[h]["vcod"] = vcod
            hd[h]["vscl"] = vscl

        def mview(kk):
            t = kk % NT
            return hd[kk // NT]["m"][:, t * S:(t + 1) * S].rearrange("i (p u e) -> i u p e", u=2, e=2)

        def mm(kq, e):
            if kq < 0 or kq >= NTILES:
                return
            st = hd[kq // NT]
            t = kq % NT
            if e == 0:
                s_new = ps_s.tile([P, S], F32, tag="s", name="s_ps")
                tl[kq] = {"s_ps": s_new}
            s_ps = tl[kq]["s_ps"]
            nc.tensor.matmul(s_ps[:], lhsT=st["qTb"][:, t, :, e], rhs=st["kTb"][:, :, e], start=(e == 0), stop=False)
            if e == 1 and kq in PEMASK:
                nc.tensor.matmul(upe(s_ps[:]), lhsT=identb[:], rhs=mview(kq), start=False, stop=False)

        def dec(kq, cs):
            if kq < 0 or kq >= NTILES:
                return
            s_ps = tl[kq]["s_ps"]
            for c in cs:
                nc.tensor.matmul(
                    s_ps[:, c * P:(c + 1) * P],
                    lhsT=dmat[:, c * P:(c + 1) * P],
                    rhs=ident32[:],
                    start=False,
                    stop=(c == NT - 1),
                    is_transpose=True,
                )

        def etr(ke, u):
            if ke < 0 or ke >= NTILES:
                return
            g, a = gof(ke)
            if a == 0 and u == 0:
                if ke == NTILES - 1:
                    eT_new = ps_s.tile([P, 1, 2, P], F32, tag="s", name="eT_ps")
                else:
                    eT_new = ps_et.tile([P, len(g), 2, P], F32, tag="et", name="eT_ps")
                pr[g]["eT_ps"] = eT_new
            words = tl[ke]["e_sb"][:].bitcast(F32)
            nc.tensor.transpose(pr[g]["eT_ps"][:, a, u, :], words[:, u * P:(u + 1) * P], ident32[:])

        def badd(kk):
            if kk < 0 or kk >= NTILES:
                return
            if kk in PEMASK:
                tl[kk]["s_src"] = tl[kk]["s_ps"]
            else:
                s_sb = wk.tile([P, S], F32, tag="s_sb", name="s_sb", bufs=5)
                nc.vector.tensor_tensor(out=upe(s_sb[:]), in0=upe(tl[kk]["s_ps"][:]), in1=mview(kk), op=ADD)
                tl[kk]["s_src"] = s_sb

        def cmax(kk):
            if kk < 0 or kk >= NTILES:
                return
            negm = wk.tile([P, 1], F32, tag="negm", name="negm", bufs=4)
            nc.vector.tensor_reduce(out=negm[:], in_=tl[kk]["s_src"][:], axis=AX_X, op=MAX, negate=True)
            tl[kk]["negm"] = negm

        def dexp(kk):
            if kk < 0 or kk >= NTILES:
                return
            g, a = gof(kk)
            if a == 0:
                rsum_new = wk.tile([P, len(g)], F32, tag="rsum", name="rsum", bufs=6)
                pr[g] = {"rsum": rsum_new}
            e_sb = wk.tile([P, S], BF16, tag="e_sb", name="e_sb", bufs=4)
            nc.scalar.activation(
                out=e_sb[:], in_=tl[kk]["s_src"][:], func=EXP, bias=tl[kk]["negm"][:], scale=1.0,
                accum_out=pr[g]["rsum"][:, a:a + 1],
            )
            tl[kk]["e_sb"] = e_sb

        def xe(g):
            w = len(g)
            grp = wk.tile([P, w * P * NT], BF16, tag="grp%d" % w, name="grp", align_bytes=64, bufs=2)
            nc.scalar.copy(
                out=grp[:].bitcast(F32).rearrange("p (a i u) -> p a i u", a=w, u=2),
                in_=pr[g]["eT_ps"][:].rearrange("p a u i -> p a i u"),
            )
            pr[g]["grp"] = grp

        def qe(g):
            w = len(g)
            ecod = wk.tile([P, w * P], U32, tag="ecod%d" % w, name="ecod", align_bytes=64, bufs=3)
            escl = wk.tile([P, w * P], U8, tag="escl%d" % w, name="escl", align_bytes=64, bufs=3)
            nc.vector.quantize_mx(out=ecod[:].bitcast(FP8X4), scales=escl[:], in_=pr[g]["grp"][:])
            rinv = wk.tile([P, w], F32, tag="rinv", name="rinv", bufs=4)
            nc.vector.reciprocal(rinv[:], pr[g]["rsum"][:])
            pr[g]["ecod"] = ecod
            pr[g]["escl"] = escl
            pr[g]["rinv"] = rinv

        def pv(g):
            w = len(g)
            st = hd[g[0] // NT]
            if g[0] >= NTILES - 4:
                o_ps = ps_s.tile([P, w, D], F32, tag="s", name="o_ps")
            else:
                o_ps = ps_o.tile([P, w, D], F32, tag="o", name="o_ps")
            for a in range(w):
                nc.tensor.matmul_mx(
                    out=o_ps[:, a, :],
                    lhsT=pr[g]["ecod"][:, a * P:(a + 1) * P].bitcast(FP8X4),
                    lhsT_scale=pr[g]["escl"][:, a * P:(a + 1) * P],
                    rhs=st["vcod"][:].bitcast(FP8X4),
                    rhs_scale=st["vscl"][:],
                    start=True,
                    stop=True,
                )
            pr[g]["o_ps"] = o_ps

        def on_vector(kk):
            return kk % 4 == 2 or (kk >= NTILES - 8 and kk % 2 == 0)

        def oex(kk):
            h = kk // NT
            t = kk % NT
            g, a = gof(kk)
            if t == 0:
                o_new = wk.tile([P, NT * D], F32, tag="o_sb", name="o_sb", bufs=3)
                hd[h]["o_sb"] = o_new
            o_sb = hd[h]["o_sb"]
            if on_vector(kk):
                nc.vector.tensor_scalar(
                    out=o_sb[:, t * D:(t + 1) * D], in0=pr[g]["o_ps"][:, a, :], scalar1=pr[g]["rinv"][:, a:a + 1],
                    scalar2=None, op0=MULT,
                )
            else:
                nc.scalar.activation(
                    out=o_sb[:, t * D:(t + 1) * D], in_=pr[g]["o_ps"][:, a, :], func=COPY,
                    scale=pr[g]["rinv"][:, a:a + 1],
                )

        def store(h, a, b):
            nc.sync.dma_start(
                out=out[h].rearrange("(p t) d -> p (t d)", t=NT)[:, a * D:b * D], in_=hd[h]["o_sb"][:, a * D:b * D]
            )

        for h, which in ((0, "k"), (0, "q"), (0, "m"), (1, "q"), (1, "k"), (0, "v"), (1, "m"), (1, "v")):
            load(h, which)
        for which in ("q", "k", "m", "v"):
            load(2, which)
        first_qk()
        for s in range(-3, NTILES + 9):
            if s >= 0 and s % 4 == 0:
                for which in ("q", "k", "m", "v"):
                    load(s // 4 + LA, which)
            if (s - 12) % 4 == 0 and (s - 12) // 4 >= 0 and (s - 12) // 4 < BH - 1:
                store((s - 12) // 4, 0, NT)
            mm(s + 3, 0)
            dec(s + 2, (0, 1))
            etr(s - 2, 0)
            mm(s + 3, 1)
            dec(s + 2, (2, 3))
            etr(s - 2, 1)
            if s == -2:
                tqk(1, "q")
            if s == -1:
                tqk(1, "k")
            if s >= 0 and s % 4 == 0:
                tqk(s // 4 + 2, "q")
            if s >= 0 and s % 4 == 2:
                tqk(s // 4 + 2, "k")
            for g in at(s, PV):
                pv(g)
            if s % 4 == 0:
                rgv(s // 4)
            for kk in at(s, OEX):
                if on_vector(kk):
                    oex(kk)
            if s + 1 in PEMASK:
                badd(s + 1)
                cmax(s + 1)
            else:
                badd(s + 1)
            if s not in PEMASK:
                cmax(s)
            if (s - 4) % 4 == 0:
                qv((s - 4) // 4)
            for g in at(s, QE):
                qe(g)
            for kk in at(s, OEX):
                if not on_vector(kk):
                    oex(kk)
            if s in PEMASK:
                dexp(s)
            if s - 1 not in PEMASK:
                dexp(s - 1)
            for g in at(s, XE):
                xe(g)
            if s == -1:
                xq(1)
            if s == 0:
                xk(1)
            if s >= 0 and s % 4 == 1:
                xq(s // 4 + 2)
            if s >= 0 and s % 4 == 3:
                xk(s // 4 + 2)
            for kk in at(s, OEX):
                if kk >= NTILES - NT:
                    store(BH - 1, kk % NT, kk % NT + 1)
